import numpy as np
import ml_dtypes

BF16 = ml_dtypes.bfloat16


def bf(x):
    return np.asarray(x, np.float32).astype(BF16)


def f32(x):
    return np.asarray(x, np.float32)


def f64(x):
    return np.asarray(x).astype(np.float64)


def striped(idx):
    return np.tile(idx.reshape(-1, 16).T, (8, 1))


D, S, H, N = 128, 512, 128, 1024
OMEGA0 = 30.0


def setup_inputs():
    bnd = 0.75 * np.sqrt(6.0 / H) / OMEGA0
    return {"table": bf(np.random.uniform(-1.0, 1.0, (D, S))), "w0": bf(np.random.uniform(-0.5 / D, 0.5 / D, (D, H))), "b0": f32(0.1 * np.random.standard_normal((H, 1)) / OMEGA0), "w1": bf(np.random.uniform(-bnd, bnd, (H, H))), "b1": f32(0.1 * np.random.standard_normal((H, 1)) / OMEGA0), "w2": bf(np.random.uniform(-bnd, bnd, (H, H))), "b2": f32(0.1 * np.random.standard_normal((H, 1)) / OMEGA0), "offs": striped(np.random.permutation(np.tile(np.arange(S), 2))[:N])}


def reference(table, w0, b0, w1, b1, w2, b2, offs):
    idx = offs[:16].T.reshape(-1)
    x = np.sin(OMEGA0 * (f64(w0).T @ f64(table)[:, idx] + f64(b0)))
    x = np.sin(OMEGA0 * (f64(w1).T @ x + f64(b1)))
    x = np.sin(OMEGA0 * (f64(w2).T @ x + f64(b2)))
    return x

@@ -1,0 +1,83 @@
+import math
+
+import concourse.mybir as mybir
+
+FLOPS = 2 * 128 * 128 * 1024 * 3
+
+P = 128
+WORDS = 512
+N = 1024
+PIECE = 512
+PIECES = N // PIECE
+LAYERS = 3
+
+OMEGA0 = 30.0
+TURNS_PER_UNIT = OMEGA0 / (2.0 * math.pi)
+UNITS_PER_TURN = 2.0 * math.pi / OMEGA0
+
+BF16 = mybir.dt.bfloat16
+F32 = mybir.dt.float32
+I32 = mybir.dt.int32
+U16 = mybir.dt.uint16
+ADD = mybir.AluOpType.add
+MULT = mybir.AluOpType.mult
+SIN = mybir.ActivationFunctionType.Sin
+
+
+def tile_implicitembedding_kernel(tc, table, w0, b0, w1, b1, w2, b2, offs, out):
+    nc = tc.nc
+    with (
+        tc.tile_pool(name="held", bufs=1) as held,
+        tc.tile_pool(name="work", bufs=2 * PIECES) as work,
+        tc.psum_pool(name="psum", bufs=LAYERS * PIECES) as psum,
+    ):
+        offsets = held.tile([P, N // 16], U16, name="offsets")
+        nc.sync.dma_start(offsets[:], offs)
+        words = held.tile([P, WORDS], BF16, name="words")
+        nc.sync.dma_start(words[:], table)
+        weights = []
+        biases = []
+        for layer, (w, b) in enumerate(((w0, b0), (w1, b1), (w2, b2))):
+            weight = held.tile([P, P], BF16, name=f"weight{layer}")
+            nc.scalar.dma_start(weight[:], w)
+            weights.append(weight)
+            bias = held.tile([P, 1], F32, name=f"bias{layer}")
+            nc.scalar.dma_start(bias[:], b)
+            biases.append(bias)
+
+        scaled_biases = []
+        for layer in range(LAYERS):
+            scaled_bias = held.tile([P, 1], F32, name=f"scaled_bias{layer}")
+            nc.vector.tensor_scalar_mul(scaled_bias[:], biases[layer][:], OMEGA0)
+            scaled_biases.append(scaled_bias)
+
+        hidden = [None] * PIECES
+        for layer in range(LAYERS):
+            for piece in range(PIECES):
+                product = psum.tile([P, PIECE], F32, name="product")
+                if layer == 0:
+                    first = piece * (PIECE // 16)
+                    moving = words[:].indirect(offsets[:, first : first + PIECE // 16])
+                else:
+                    moving = hidden[piece][:]
+                nc.tensor.matmul(product[:], weights[layer][:], moving, start=True, stop=True)
+
+                turns = work.tile([P, PIECE], I32, name="turns")
+                nc.vector.tensor_scalar(
+                    turns[:], product[:], biases[layer][:], TURNS_PER_UNIT, ADD, MULT
+                )
+                reduced = work.tile([P, PIECE], F32, name="reduced")
+                nc.vector.scalar_tensor_tensor(
+                    reduced[:], turns[:], -UNITS_PER_TURN, product[:], MULT, ADD
+                )
+
+                if layer < LAYERS - 1:
+                    sine = work.tile([P, PIECE], BF16, name="sine")
+                    hidden[piece] = sine
+                else:
+                    sine = work.tile([P, PIECE], F32, name="result")
+                nc.scalar.activation(
+                    sine[:], reduced[:], SIN, bias=scaled_biases[layer][:], scale=OMEGA0
+                )
+                if layer == LAYERS - 1:
+                    nc.sync.dma_start(out[:, piece * PIECE : (piece + 1) * PIECE], sine[:])

@@ -7,7 +7,8 @@ FLOPS = 2 * 128 * 128 * 1024 * 3
 P = 128
 WORDS = 512
 N = 1024
-PIECE = 512
+PIECE = 256
+PSUM_BANKS = 8
 PIECES = N // PIECE
 LAYERS = 3
 
@@ -29,7 +30,7 @@ def tile_implicitembedding_kernel(tc, table, w0, b0, w1, b1, w2, b2, offs, out):
     with (
         tc.tile_pool(name="held", bufs=1) as held,
         tc.tile_pool(name="work", bufs=2 * PIECES) as work,
-        tc.psum_pool(name="psum", bufs=LAYERS * PIECES) as psum,
+        tc.psum_pool(name="psum", bufs=PSUM_BANKS) as psum,
     ):
         offsets = held.tile([P, N // 16], U16, name="offsets")
         nc.sync.dma_start(offsets[:], offs)

@@ -8,13 +8,12 @@ P = 128
 WORDS = 512
 N = 1024
 PIECE = 256
-PSUM_BANKS = 8
 PIECES = N // PIECE
 LAYERS = 3
+PSUM_BANKS = 8
 
 OMEGA0 = 30.0
-TURNS_PER_UNIT = OMEGA0 / (2.0 * math.pi)
-UNITS_PER_TURN = 2.0 * math.pi / OMEGA0
+TWO_PI = 2.0 * math.pi
 
 BF16 = mybir.dt.bfloat16
 F32 = mybir.dt.float32
@@ -54,6 +53,7 @@ def tile_implicitembedding_kernel(tc, table, w0, b0, w1, b1, w2, b2, offs, out):
 
         hidden = [None] * PIECES
         for layer in range(LAYERS):
+            products = []
             for piece in range(PIECES):
                 product = psum.tile([P, PIECE], F32, name="product")
                 if layer == 0:
@@ -62,23 +62,29 @@ def tile_implicitembedding_kernel(tc, table, w0, b0, w1, b1, w2, b2, offs, out):
                 else:
                     moving = hidden[piece][:]
                 nc.tensor.matmul(product[:], weights[layer][:], moving, start=True, stop=True)
+                products.append(product)
 
-                turns = work.tile([P, PIECE], I32, name="turns")
-                nc.vector.tensor_scalar(
-                    turns[:], product[:], biases[layer][:], TURNS_PER_UNIT, ADD, MULT
-                )
-                reduced = work.tile([P, PIECE], F32, name="reduced")
-                nc.vector.scalar_tensor_tensor(
-                    reduced[:], turns[:], -UNITS_PER_TURN, product[:], MULT, ADD
-                )
-
-                if layer < LAYERS - 1:
-                    sine = work.tile([P, PIECE], BF16, name="sine")
-                    hidden[piece] = sine
-                else:
-                    sine = work.tile([P, PIECE], F32, name="result")
-                nc.scalar.activation(
-                    sine[:], reduced[:], SIN, bias=scaled_biases[layer][:], scale=OMEGA0
-                )
-                if layer == LAYERS - 1:
-                    nc.sync.dma_start(out[:, piece * PIECE : (piece + 1) * PIECE], sine[:])
+            whole_turns = []
+            for step in range(PIECES + 1):
+                if step < PIECES:
+                    turns = work.tile([P, PIECE], I32, name="turns")
+                    nc.vector.tensor_scalar(
+                        turns[:], products[step][:], biases[layer][:], OMEGA0 / TWO_PI, ADD, MULT
+                    )
+                    whole_turns.append(turns)
+                if step > 0:
+                    piece = step - 1
+                    reduced = work.tile([P, PIECE], F32, name="reduced")
+                    nc.vector.scalar_tensor_tensor(
+                        reduced[:], whole_turns[piece][:], -TWO_PI / OMEGA0, products[piece][:], MULT, ADD
+                    )
+                    if layer < LAYERS - 1:
+                        sine = work.tile([P, PIECE], BF16, name="sine")
+                        hidden[piece] = sine
+                    else:
+                        sine = work.tile([P, PIECE], F32, name="result")
+                    nc.scalar.activation(
+                        sine[:], reduced[:], SIN, bias=scaled_biases[layer][:], scale=OMEGA0
+                    )
+                    if layer == LAYERS - 1:
+                        nc.sync.dma_start(out[:, piece * PIECE : (piece + 1) * PIECE], sine[:])

@@ -29,31 +29,41 @@ def tile_implicitembedding_kernel(tc, table, w0, b0, w1, b1, w2, b2, offs, out):
     with (
         tc.tile_pool(name="held", bufs=1) as held,
         tc.tile_pool(name="work", bufs=2 * PIECES) as work,
-        tc.psum_pool(name="psum", bufs=PSUM_BANKS) as psum,
+        tc.psum_pool(name="psum_held", bufs=1) as psum_held,
+        tc.psum_pool(name="psum", bufs=PSUM_BANKS - 1) as psum,
     ):
         offsets = held.tile([P, N // 16], U16, name="offsets")
         nc.sync.dma_start(offsets[:], offs)
         words = held.tile([P, WORDS], BF16, name="words")
         nc.sync.dma_start(words[:], table)
+        bias_rows = held.tile([1, LAYERS * P], F32, name="bias_rows")
         weights = []
-        biases = []
         for layer, (w, b) in enumerate(((w0, b0), (w1, b1), (w2, b2))):
             weight = held.tile([P, P], BF16, name=f"weight{layer}")
             nc.scalar.dma_start(weight[:], w)
             weights.append(weight)
-            bias = held.tile([P, 1], F32, name=f"bias{layer}")
-            nc.scalar.dma_start(bias[:], b)
-            biases.append(bias)
+            nc.scalar.dma_start(
+                bias_rows[:, layer * P : (layer + 1) * P], b.rearrange("h one -> one h")
+            )
 
-        scaled_biases = []
+        one = held.tile([1, 1], F32, name="one")
+        nc.vector.memset(one[:], 1.0)
+        bias_columns = psum_held.tile([P, LAYERS], F32, name="bias_columns")
         for layer in range(LAYERS):
-            scaled_bias = held.tile([P, 1], F32, name=f"scaled_bias{layer}")
-            nc.vector.tensor_scalar_mul(scaled_bias[:], biases[layer][:], OMEGA0)
-            scaled_biases.append(scaled_bias)
+            nc.tensor.matmul(
+                bias_columns[:, layer : layer + 1],
+                bias_rows[:, layer * P : (layer + 1) * P],
+                one[:],
+                start=True,
+                stop=True,
+            )
+        biases = held.tile([P, LAYERS], F32, name="biases")
+        nc.vector.tensor_copy(biases[:], bias_columns[:])
+        scaled_biases = held.tile([P, LAYERS], F32, name="scaled_biases")
+        nc.vector.tensor_scalar_mul(scaled_biases[:], bias_columns[:], OMEGA0)
 
         hidden = [None] * PIECES
         for layer in range(LAYERS):
-            products = []
             for piece in range(PIECES):
                 product = psum.tile([P, PIECE], F32, name="product")
                 if layer == 0:
@@ -62,29 +72,27 @@ def tile_implicitembedding_kernel(tc, table, w0, b0, w1, b1, w2, b2, offs, out):
                 else:
                     moving = hidden[piece][:]
                 nc.tensor.matmul(product[:], weights[layer][:], moving, start=True, stop=True)
-                products.append(product)
 
-            whole_turns = []
-            for step in range(PIECES + 1):
-                if step < PIECES:
-                    turns = work.tile([P, PIECE], I32, name="turns")
-                    nc.vector.tensor_scalar(
-                        turns[:], products[step][:], biases[layer][:], OMEGA0 / TWO_PI, ADD, MULT
-                    )
-                    whole_turns.append(turns)
-                if step > 0:
-                    piece = step - 1
-                    reduced = work.tile([P, PIECE], F32, name="reduced")
-                    nc.vector.scalar_tensor_tensor(
-                        reduced[:], whole_turns[piece][:], -TWO_PI / OMEGA0, products[piece][:], MULT, ADD
-                    )
-                    if layer < LAYERS - 1:
-                        sine = work.tile([P, PIECE], BF16, name="sine")
-                        hidden[piece] = sine
-                    else:
-                        sine = work.tile([P, PIECE], F32, name="result")
-                    nc.scalar.activation(
-                        sine[:], reduced[:], SIN, bias=scaled_biases[layer][:], scale=OMEGA0
-                    )
-                    if layer == LAYERS - 1:
-                        nc.sync.dma_start(out[:, piece * PIECE : (piece + 1) * PIECE], sine[:])
+                turns = work.tile([P, PIECE], I32, name="turns")
+                nc.vector.tensor_scalar(
+                    turns[:], product[:], biases[:, layer : layer + 1], OMEGA0 / TWO_PI, ADD, MULT
+                )
+                reduced = work.tile([P, PIECE], F32, name="reduced")
+                nc.vector.scalar_tensor_tensor(
+                    reduced[:], turns[:], -TWO_PI / OMEGA0, product[:], MULT, ADD
+                )
+
+                if layer < LAYERS - 1:
+                    sine = work.tile([P, PIECE], BF16, name="sine")
+                    hidden[piece] = sine
+                else:
+                    sine = work.tile([P, PIECE], F32, name="result")
+                nc.scalar.activation(
+                    sine[:],
+                    reduced[:],
+                    SIN,
+                    bias=scaled_biases[:, layer : layer + 1],
+                    scale=OMEGA0,
+                )
+                if layer == LAYERS - 1:
+                    nc.sync.dma_start(out[:, piece * PIECE : (piece + 1) * PIECE], sine[:])

@@ -7,13 +7,14 @@ FLOPS = 2 * 128 * 128 * 1024 * 3
 P = 128
 WORDS = 512
 N = 1024
-PIECE = 256
+PIECE = 128
+PSUM_BANKS = 8
 PIECES = N // PIECE
 LAYERS = 3
-PSUM_BANKS = 8
 
 OMEGA0 = 30.0
-TWO_PI = 2.0 * math.pi
+TURNS_PER_UNIT = OMEGA0 / (2.0 * math.pi)
+UNITS_PER_TURN = 2.0 * math.pi / OMEGA0
 
 BF16 = mybir.dt.bfloat16
 F32 = mybir.dt.float32
@@ -29,38 +30,27 @@ def tile_implicitembedding_kernel(tc, table, w0, b0, w1, b1, w2, b2, offs, out):
     with (
         tc.tile_pool(name="held", bufs=1) as held,
         tc.tile_pool(name="work", bufs=2 * PIECES) as work,
-        tc.psum_pool(name="psum_held", bufs=1) as psum_held,
-        tc.psum_pool(name="psum", bufs=PSUM_BANKS - 1) as psum,
+        tc.psum_pool(name="psum", bufs=PSUM_BANKS) as psum,
     ):
         offsets = held.tile([P, N // 16], U16, name="offsets")
         nc.sync.dma_start(offsets[:], offs)
         words = held.tile([P, WORDS], BF16, name="words")
         nc.sync.dma_start(words[:], table)
-        bias_rows = held.tile([1, LAYERS * P], F32, name="bias_rows")
         weights = []
+        biases = []
         for layer, (w, b) in enumerate(((w0, b0), (w1, b1), (w2, b2))):
             weight = held.tile([P, P], BF16, name=f"weight{layer}")
             nc.scalar.dma_start(weight[:], w)
             weights.append(weight)
-            nc.scalar.dma_start(
-                bias_rows[:, layer * P : (layer + 1) * P], b.rearrange("h one -> one h")
-            )
+            bias = held.tile([P, 1], F32, name=f"bias{layer}")
+            nc.scalar.dma_start(bias[:], b)
+            biases.append(bias)
 
-        one = held.tile([1, 1], F32, name="one")
-        nc.vector.memset(one[:], 1.0)
-        bias_columns = psum_held.tile([P, LAYERS], F32, name="bias_columns")
+        scaled_biases = []
         for layer in range(LAYERS):
-            nc.tensor.matmul(
-                bias_columns[:, layer : layer + 1],
-                bias_rows[:, layer * P : (layer + 1) * P],
-                one[:],
-                start=True,
-                stop=True,
-            )
-        biases = held.tile([P, LAYERS], F32, name="biases")
-        nc.vector.tensor_copy(biases[:], bias_columns[:])
-        scaled_biases = held.tile([P, LAYERS], F32, name="scaled_biases")
-        nc.vector.tensor_scalar_mul(scaled_biases[:], bias_columns[:], OMEGA0)
+            scaled_bias = held.tile([P, 1], F32, name=f"scaled_bias{layer}")
+            nc.vector.tensor_scalar_mul(scaled_bias[:], biases[layer][:], OMEGA0)
+            scaled_biases.append(scaled_bias)
 
         hidden = [None] * PIECES
         for layer in range(LAYERS):
@@ -75,11 +65,11 @@ def tile_implicitembedding_kernel(tc, table, w0, b0, w1, b1, w2, b2, offs, out):
 
                 turns = work.tile([P, PIECE], I32, name="turns")
                 nc.vector.tensor_scalar(
-                    turns[:], product[:], biases[:, layer : layer + 1], OMEGA0 / TWO_PI, ADD, MULT
+                    turns[:], product[:], biases[layer][:], TURNS_PER_UNIT, ADD, MULT
                 )
                 reduced = work.tile([P, PIECE], F32, name="reduced")
                 nc.vector.scalar_tensor_tensor(
-                    reduced[:], turns[:], -TWO_PI / OMEGA0, product[:], MULT, ADD
+                    reduced[:], turns[:], -UNITS_PER_TURN, product[:], MULT, ADD
                 )
 
                 if layer < LAYERS - 1:
@@ -88,11 +78,7 @@ def tile_implicitembedding_kernel(tc, table, w0, b0, w1, b1, w2, b2, offs, out):
                 else:
                     sine = work.tile([P, PIECE], F32, name="result")
                 nc.scalar.activation(
-                    sine[:],
-                    reduced[:],
-                    SIN,
-                    bias=scaled_biases[:, layer : layer + 1],
-                    scale=OMEGA0,
+                    sine[:], reduced[:], SIN, bias=scaled_biases[layer][:], scale=OMEGA0
                 )
                 if layer == LAYERS - 1:
                     nc.sync.dma_start(out[:, piece * PIECE : (piece + 1) * PIECE], sine[:])

@@ -1,5 +1,3 @@
-import math
-
 import concourse.mybir as mybir
 
 FLOPS = 2 * 128 * 128 * 1024 * 3
@@ -13,15 +11,10 @@ PIECES = N // PIECE
 LAYERS = 3
 
 OMEGA0 = 30.0
-TURNS_PER_UNIT = OMEGA0 / (2.0 * math.pi)
-UNITS_PER_TURN = 2.0 * math.pi / OMEGA0
 
 BF16 = mybir.dt.bfloat16
 F32 = mybir.dt.float32
-I32 = mybir.dt.int32
 U16 = mybir.dt.uint16
-ADD = mybir.AluOpType.add
-MULT = mybir.AluOpType.mult
 SIN = mybir.ActivationFunctionType.Sin
 
 
@@ -63,22 +56,13 @@ def tile_implicitembedding_kernel(tc, table, w0, b0, w1, b1, w2, b2, offs, out):
                     moving = hidden[piece][:]
                 nc.tensor.matmul(product[:], weights[layer][:], moving, start=True, stop=True)
 
-                turns = work.tile([P, PIECE], I32, name="turns")
-                nc.vector.tensor_scalar(
-                    turns[:], product[:], biases[layer][:], TURNS_PER_UNIT, ADD, MULT
-                )
-                reduced = work.tile([P, PIECE], F32, name="reduced")
-                nc.vector.scalar_tensor_tensor(
-                    reduced[:], turns[:], -UNITS_PER_TURN, product[:], MULT, ADD
-                )
-
                 if layer < LAYERS - 1:
                     sine = work.tile([P, PIECE], BF16, name="sine")
                     hidden[piece] = sine
                 else:
                     sine = work.tile([P, PIECE], F32, name="result")
                 nc.scalar.activation(
-                    sine[:], reduced[:], SIN, bias=scaled_biases[layer][:], scale=OMEGA0
+                    sine[:], product[:], SIN, bias=scaled_biases[layer][:], scale=OMEGA0
                 )
                 if layer == LAYERS - 1:
                     nc.sync.dma_start(out[:, piece * PIECE : (piece + 1) * PIECE], sine[:])

@@ -39,6 +39,11 @@ def tile_implicitembedding_kernel(tc, table, w0, b0, w1, b1, w2, b2, offs, out):
             nc.scalar.dma_start(bias[:], b)
             biases.append(bias)
 
+        scratch = held.tile([P, 1], F32, name="scratch")
+        nc.vector.memset(scratch[:], 0.0)
+        warmed = held.tile([P, 1], F32, name="warmed")
+        nc.scalar.activation(warmed[:], scratch[:], SIN)
+
         scaled_biases = []
         for layer in range(LAYERS):
             scaled_bias = held.tile([P, 1], F32, name=f"scaled_bias{layer}")

@@ -5,7 +5,7 @@ FLOPS = 2 * 128 * 128 * 1024 * 3
 P = 128
 WORDS = 512
 N = 1024
-PIECE = 128
+PIECE = 256
 PSUM_BANKS = 8
 PIECES = N // PIECE
 LAYERS = 3

@@ -33,10 +33,10 @@ def tile_implicitembedding_kernel(tc, table, w0, b0, w1, b1, w2, b2, offs, out):
         biases = []
         for layer, (w, b) in enumerate(((w0, b0), (w1, b1), (w2, b2))):
             weight = held.tile([P, P], BF16, name=f"weight{layer}")
-            nc.scalar.dma_start(weight[:], w)
+            nc.sync.dma_start(weight[:], w)
             weights.append(weight)
             bias = held.tile([P, 1], F32, name=f"bias{layer}")
-            nc.scalar.dma_start(bias[:], b)
+            nc.sync.dma_start(bias[:], b)
             biases.append(bias)
 
         scratch = held.tile([P, 1], F32, name="scratch")

import concourse.mybir as mybir

FLOPS = 2 * 128 * 128 * 1024 * 3

P = 128
WORDS = 512
N = 1024
PIECE = 256
PSUM_BANKS = 8
PIECES = N // PIECE
LAYERS = 3

OMEGA0 = 30.0

BF16 = mybir.dt.bfloat16
F32 = mybir.dt.float32
U16 = mybir.dt.uint16
SIN = mybir.ActivationFunctionType.Sin


def tile_implicitembedding_kernel(tc, table, w0, b0, w1, b1, w2, b2, offs, out):
    nc = tc.nc
    with (
        tc.tile_pool(name="held", bufs=1) as held,
        tc.tile_pool(name="work", bufs=2 * PIECES) as work,
        tc.psum_pool(name="psum", bufs=PSUM_BANKS) as psum,
    ):
        offsets = held.tile([P, N // 16], U16, name="offsets")
        nc.sync.dma_start(offsets[:], offs)
        words = held.tile([P, WORDS], BF16, name="words")
        nc.sync.dma_start(words[:], table)
        weights = []
        biases = []
        for layer, (w, b) in enumerate(((w0, b0), (w1, b1), (w2, b2))):
            weight = held.tile([P, P], BF16, name=f"weight{layer}")
            nc.sync.dma_start(weight[:], w)
            weights.append(weight)
            bias = held.tile([P, 1], F32, name=f"bias{layer}")
            nc.sync.dma_start(bias[:], b)
            biases.append(bias)

        scratch = held.tile([P, 1], F32, name="scratch")
        nc.vector.memset(scratch[:], 0.0)
        warmed = held.tile([P, 1], F32, name="warmed")
        nc.scalar.activation(warmed[:], scratch[:], SIN)

        scaled_biases = []
        for layer in range(LAYERS):
            scaled_bias = held.tile([P, 1], F32, name=f"scaled_bias{layer}")
            nc.vector.tensor_scalar_mul(scaled_bias[:], biases[layer][:], OMEGA0)
            scaled_biases.append(scaled_bias)

        hidden = [None] * PIECES
        for layer in range(LAYERS):
            for piece in range(PIECES):
                product = psum.tile([P, PIECE], F32, name="product")
                if layer == 0:
                    first = piece * (PIECE // 16)
                    moving = words[:].indirect(offsets[:, first : first + PIECE // 16])
                else:
                    moving = hidden[piece][:]
                nc.tensor.matmul(product[:], weights[layer][:], moving, start=True, stop=True)

                if layer < LAYERS - 1:
                    sine = work.tile([P, PIECE], BF16, name="sine")
                    hidden[piece] = sine
                else:
                    sine = work.tile([P, PIECE], F32, name="result")
                nc.scalar.activation(
                    sine[:], product[:], SIN, bias=scaled_biases[layer][:], scale=OMEGA0
                )
                if layer == LAYERS - 1:
                    nc.sync.dma_start(out[:, piece * PIECE : (piece + 1) * PIECE], sine[:])
